import numpy as np
import ml_dtypes


def mxq(x, axis, fmt="e4m3"):
    dtype, down = {"e4m3": (ml_dtypes.float8_e4m3fn, 7), "e5m2": (ml_dtypes.float8_e5m2, 14)}[fmt]
    v = np.moveaxis(np.asarray(x, np.float32).astype(ml_dtypes.bfloat16).astype(np.float64), axis, -1)
    blocks = v.reshape(v.shape[:-1] + (-1, 32))
    amax = np.abs(blocks).max(-1, keepdims=True)
    byte = np.maximum(np.where(amax > 0, np.frexp(amax)[1] - 1 + 127, 0) - down, 1)
    scale = np.exp2(byte - 127.0)
    codes = (blocks / scale).astype(np.float32).astype(dtype).astype(np.float64)
    return np.moveaxis((codes * scale).reshape(v.shape), -1, axis)


WIDE = False


def mx_kscale(k):
    if not WIDE:
        return np.ones(k)
    levels = np.array([10, -10, 5, -5, 0])
    a = np.random.permutation(np.resize(levels, k // 512 * 4)).reshape(k // 512, 4)
    idx = np.arange(k)
    return np.exp2(a[idx // 512, idx % 128 // 32])


BF16 = ml_dtypes.bfloat16


def bf(x):
    return np.asarray(x, np.float32).astype(BF16)


def f64(x):
    return np.asarray(x).astype(np.float64)


N, F_IN, F_OUT = 512, 1024, 128


def setup_inputs():
    s = mx_kscale(F_IN)
    return {"input": bf(np.random.standard_normal((N, F_IN)) * s),
            "adj": bf(np.random.uniform(0.0, 1.0, (N, N))),
            "weight": bf(np.random.uniform(-1.0, 1.0, (F_IN, F_OUT)) * 0.35 * np.sqrt(N / F_IN) / s[:, None]),
            "b": bf(np.random.uniform(-1.0, 1.0, F_OUT) * 0.2)}


def reference(input, adj, weight, b):
    adj = f64(adj)
    n = adj.shape[0]
    degree = np.sum(adj, axis=1)
    A_tilde = 2.0 * np.eye(n) - adj
    d_inv_sqrt = 1.0 / np.sqrt(2.0 + degree)
    L_sharpen = d_inv_sqrt[:, None] * A_tilde * d_inv_sqrt[None, :]
    support = mxq(f64(input), 1, "e4m3") @ mxq(f64(weight), 0, "e4m3")
    out = (mxq(L_sharpen, 1, "e4m3") @ mxq(support, 0, "e4m3")) + f64(b)
    return np.maximum(out, 0.0)

@@ -1,0 +1,177 @@
+from contextlib import ExitStack
+
+import concourse.mybir as mybir
+from concourse.masks import make_identity
+
+F32 = mybir.dt.float32
+BF16 = mybir.dt.bfloat16
+U32 = mybir.dt.uint32
+U8 = mybir.dt.uint8
+FP8X4 = mybir.dt.float8_e4m3fn_x4
+ACT = mybir.ActivationFunctionType
+ALU = mybir.AluOpType
+
+P = 128
+PACK = 4
+K_PASS = P * PACK
+NODES = 512
+F_IN = 1024
+F_OUT = 128
+TILES = NODES // P
+PASSES = F_IN // K_PASS
+HALF = 2
+
+FLOPS = 2 * NODES * F_IN * F_OUT + 2 * NODES * NODES * F_OUT
+
+
+def tile_graphconvolution_s_kernel(tc, x, adj, weight, b, out):
+    nc = tc.nc
+    with ExitStack() as stack:
+        const = stack.enter_context(tc.tile_pool(name="const", bufs=1))
+        keep = stack.enter_context(tc.tile_pool(name="keep", bufs=1))
+        ps_x = stack.enter_context(tc.psum_pool(name="ps_x", bufs=3))
+        ps_l = stack.enter_context(tc.psum_pool(name="ps_l", bufs=2))
+        ps_one = stack.enter_context(tc.psum_pool(name="ps_one", bufs=1))
+
+        adj_rows = adj.rearrange("(t p) j -> p t j", p=P)
+        adj_sb = keep.tile([P, TILES, NODES], BF16)
+        for h in range(2):
+            nc.sync.dma_start(out=adj_sb[:, 2 * h : 2 * h + 2, :], in_=adj_rows[:, 2 * h : 2 * h + 2, :])
+        w_sb = keep.tile([P, PASSES, PACK, F_OUT], BF16)
+        nc.sync.dma_start(
+            out=w_sb[:].rearrange("q g (u e) f -> q (g u) (e f)", e=2),
+            in_=weight.rearrange("(c q e) f -> q c (e f)", q=P, e=2),
+        )
+        x_rows = x.rearrange("(t p) k -> p t k", p=P)
+        x_sb = []
+        for t in range(TILES):
+            x_t = keep.tile([P, F_IN], BF16, name="x%d" % t)
+            nc.sync.dma_start(out=x_t[:], in_=x_rows[:, t, :])
+            x_sb.append(x_t)
+        bias_row = const.tile([P, F_OUT], BF16)
+        nc.vector.memset(bias_row[:], 0.0)
+        nc.scalar.dma_start(out=bias_row[0:1, :], in_=b.rearrange("(o f) -> o f", o=1))
+
+        ident = const.tile([P, P], F32)
+        make_identity(nc, ident[:])
+        ones = const.tile([P, P], BF16)
+        nc.vector.memset(ones[:], 1.0)
+        warm = const.tile([P, 1], F32)
+        nc.vector.memset(warm[:], 1.0)
+        nc.scalar.activation(out=warm[:], in_=warm[:], func=ACT.Abs_reciprocal_sqrt)
+
+        bias_ps = ps_one.tile([P, F_OUT], F32)
+        nc.tensor.matmul(out=bias_ps[:], lhsT=ones[:], rhs=bias_row[:], start=True, stop=True)
+        bias_sb = const.tile([P, F_OUT], F32)
+        nc.scalar.copy(out=bias_sb[:], in_=bias_ps[:])
+
+        w_grouped = keep.tile([P, PASSES, F_OUT, PACK], BF16, align_bytes=64)
+        nc.vector.tensor_copy(out=w_grouped[:], in_=w_sb[:].rearrange("q g t f -> q g f t"))
+        w_codes = keep.tile([P, PASSES, F_OUT], U32, align_bytes=64)
+        w_scales = keep.tile([P, PASSES, F_OUT], U8, align_bytes=64)
+        nc.vector.quantize_mx(
+            out=w_codes[:].rearrange("q g f -> q (g f)").bitcast(FP8X4),
+            scales=w_scales[:].rearrange("q g f -> q (g f)"),
+            in_=w_grouped[:].rearrange("q g f t -> q (g f t)"),
+        )
+
+        sharp = []
+        for t in range(TILES):
+            sharp.append(keep.tile([P, NODES], F32, name="sharp%d" % t))
+        neg_deg_v = keep.tile([P, 2], F32)
+        neg_deg_s = keep.tile([P, 2], F32)
+        for t in range(2):
+            nc.vector.tensor_scalar(
+                out=sharp[t][:], in0=adj_sb[:, t, :], scalar1=-1.0, scalar2=None,
+                op0=ALU.mult, op1=ALU.add, accum_out=neg_deg_v[:, t : t + 1],
+            )
+        for t in range(2, TILES):
+            nc.scalar.activation(
+                out=sharp[t][:], in_=adj_sb[:, t, :], func=ACT.Copy, scale=-1.0,
+                accum_out=neg_deg_s[:, t - 2 : t - 1],
+            )
+        for t in range(TILES):
+            diag = sharp[t][:, t * P : (t + 1) * P]
+            nc.vector.scalar_tensor_tensor(
+                out=diag, in0=ident[:], scalar=2.0, in1=diag, op0=ALU.mult, op1=ALU.add
+            )
+        d = keep.tile([P, TILES], F32)
+        nc.scalar.activation(out=d[:, 0:2], in_=neg_deg_v[:], func=ACT.Abs_reciprocal_sqrt, bias=2.0, scale=-1.0)
+        nc.scalar.activation(out=d[:, 2:4], in_=neg_deg_s[:], func=ACT.Abs_reciprocal_sqrt, bias=2.0, scale=-1.0)
+
+        l_codes = keep.tile([P, TILES, P], U32, align_bytes=64)
+        l_scales = keep.tile([P, TILES, P], U8, align_bytes=64)
+        for t in range(TILES):
+            nc.vector.tensor_scalar(
+                out=sharp[t][:], in0=sharp[t][:], scalar1=d[:, t : t + 1], scalar2=None, op0=ALU.mult
+            )
+            flipped = ps_l.tile([P, PACK, P], F32)
+            for u in range(PACK):
+                nc.tensor.transpose(flipped[:, u, :], sharp[t][:, u * P : (u + 1) * P], ident[:])
+            l_grouped = keep.tile([P, P, PACK], BF16, name="l_grouped%d" % t, align_bytes=64)
+            nc.vector.tensor_tensor(
+                out=l_grouped[:],
+                in0=flipped[:].rearrange("p u i -> p i u"),
+                in1=d[:].unsqueeze(1).to_broadcast([P, P, PACK]),
+                op=ALU.mult,
+            )
+            nc.vector.quantize_mx(
+                out=l_codes[:, t, :].bitcast(FP8X4),
+                scales=l_scales[:, t, :],
+                in_=l_grouped[:].rearrange("p i u -> p (i u)"),
+            )
+
+        x_codes = keep.tile([P, TILES, PASSES, P], U32, align_bytes=64)
+        x_scales = keep.tile([P, TILES, PASSES, P], U8, align_bytes=64)
+        for t in range(TILES):
+            x_words = x_sb[t][:].bitcast(F32)
+            turned = ps_x.tile([P, PASSES * HALF, P], F32)
+            for c in range(PASSES * HALF):
+                nc.tensor.transpose(turned[:, c, :], x_words[:, c * P : (c + 1) * P], ident[:])
+            x_grouped = keep.tile([P, PASSES, P, HALF], F32, name="x_grouped%d" % t, align_bytes=64)
+            nc.scalar.copy(out=x_grouped[:], in_=turned[:].rearrange("p (g u) n -> p g n u", u=HALF))
+            nc.vector.quantize_mx(
+                out=x_codes[:, t, :, :].rearrange("p g n -> p (g n)").bitcast(FP8X4),
+                scales=x_scales[:, t, :, :].rearrange("p g n -> p (g n)"),
+                in_=x_grouped[:].rearrange("p g n u -> p (g n u)").bitcast(BF16),
+            )
+
+        support = ps_one.tile([P, TILES, F_OUT], F32)
+        for t in range(TILES):
+            for g in range(PASSES):
+                nc.tensor.matmul_mx(
+                    out=support[:, t, :],
+                    lhsT=x_codes[:, t, g, :].bitcast(FP8X4),
+                    lhsT_scale=x_scales[:, t, g, :],
+                    rhs=w_codes[:, g, :].bitcast(FP8X4),
+                    rhs_scale=w_scales[:, g, :],
+                    start=(g == 0),
+                    stop=(g == PASSES - 1),
+                )
+        s_grouped = keep.tile([P, F_OUT, PACK], BF16, align_bytes=64)
+        nc.scalar.copy(out=s_grouped[:], in_=support[:].rearrange("p t f -> p f t"))
+        s_codes = keep.tile([P, F_OUT], U32, align_bytes=64)
+        s_scales = keep.tile([P, F_OUT], U8, align_bytes=64)
+        nc.vector.quantize_mx(
+            out=s_codes[:].bitcast(FP8X4),
+            scales=s_scales[:],
+            in_=s_grouped[:].rearrange("p f t -> p (f t)"),
+        )
+
+        product = ps_one.tile([P, TILES, F_OUT], F32)
+        for t in range(TILES):
+            nc.tensor.matmul_mx(
+                out=product[:, t, :],
+                lhsT=l_codes[:, t, :].bitcast(FP8X4),
+                lhsT_scale=l_scales[:, t, :],
+                rhs=s_codes[:].bitcast(FP8X4),
+                rhs_scale=s_scales[:],
+                start=True,
+                stop=True,
+            )
+        result = keep.tile([P, TILES, F_OUT], F32)
+        nc.vector.tensor_tensor(
+            out=result[:], in0=product[:], in1=bias_sb[:].unsqueeze(1).to_broadcast([P, TILES, F_OUT]), op=ALU.add
+        )
+        nc.vector.tensor_scalar_max(out=result[:], in0=result[:], scalar1=0.0)
+        nc.sync.dma_start(out=out.rearrange("(t p) f -> p t f", p=P), in_=result[:])

@@ -30,24 +30,98 @@ def tile_graphconvolution_s_kernel(tc, x, adj, weight, b, out):
         const = stack.enter_context(tc.tile_pool(name="const", bufs=1))
         keep = stack.enter_context(tc.tile_pool(name="keep", bufs=1))
         ps_x = stack.enter_context(tc.psum_pool(name="ps_x", bufs=3))
-        ps_l = stack.enter_context(tc.psum_pool(name="ps_l", bufs=2))
+        ps_l = stack.enter_context(tc.psum_pool(name="ps_l", bufs=3))
         ps_one = stack.enter_context(tc.psum_pool(name="ps_one", bufs=1))
+        stack.enter_context(tc.manual_schedule())
+
+        adj_sb = keep.tile([P, TILES, NODES], BF16)
+        w_sb = keep.tile([P, PASSES, PACK, F_OUT], BF16)
+        x_sb = [keep.tile([P, F_IN], BF16, name="x%d" % t) for t in range(TILES)]
+        sharp = keep.tile([P, TILES * (NODES + P)], F32)
+        neg_deg = keep.tile([P, 2, 8], F32)
+        d = keep.tile([P, TILES], F32)
+        w_grouped = keep.tile([P, PASSES, F_OUT, PACK], BF16, align_bytes=64)
+        w_codes = keep.tile([P, PASSES, F_OUT], U32, align_bytes=64)
+        w_scales = keep.tile([P, PASSES, F_OUT], U8, align_bytes=64)
+        x_grouped = [keep.tile([P, PASSES, P, HALF], F32, name="x_grouped%d" % t, align_bytes=64) for t in range(TILES)]
+        x_codes = keep.tile([P, TILES, PASSES, P], U32, align_bytes=64)
+        x_scales = keep.tile([P, TILES, PASSES, P], U8, align_bytes=64)
+        l_grouped = [keep.tile([P, P, PACK], BF16, name="l_grouped%d" % t, align_bytes=64) for t in range(TILES)]
+        l_codes = keep.tile([P, TILES, P], U32, align_bytes=64)
+        l_scales = keep.tile([P, TILES, P], U8, align_bytes=64)
+        turned = {}
+        flipped = {}
+
+        def row_tile(t):
+            return sharp[:, t * NODES : (t + 1) * NODES]
+
+        def negate_and_sum(t):
+            if t % 2 == 0:
+                nc.vector.tensor_scalar(
+                    out=row_tile(t), in0=adj_sb[:, t, :], scalar1=-1.0, scalar2=None,
+                    op0=ALU.mult, op1=ALU.add, accum_out=neg_deg[:, 0, t // 2 : t // 2 + 1],
+                )
+            else:
+                nc.scalar.activation(
+                    out=row_tile(t), in_=adj_sb[:, t, :], func=ACT.Copy, scale=-1.0,
+                    accum_out=neg_deg[:, 1, t // 2 : t // 2 + 1],
+                )
+
+        def scale_rows(t):
+            if t % 2 == 0:
+                nc.scalar.activation(out=row_tile(t), in_=row_tile(t), func=ACT.Copy, scale=d[:, t : t + 1])
+            else:
+                nc.gpsimd.tensor_scalar(
+                    out=row_tile(t), in0=row_tile(t), scalar1=d[:, t : t + 1], scalar2=1.0,
+                    op0=ALU.mult, op1=ALU.mult,
+                )
+
+        def flip_rows(t):
+            flipped[t] = ps_l.tile([P, PACK, P], F32, name="flipped")
+            for u in range(PACK):
+                nc.tensor.transpose(flipped[t][:, u, :], row_tile(t)[:, u * P : (u + 1) * P], ident[:])
+
+        def scale_columns(t):
+            nc.vector.tensor_tensor(
+                out=l_grouped[t][:],
+                in0=flipped[t][:].rearrange("p u i -> p i u"),
+                in1=d[:].unsqueeze(1).to_broadcast([P, P, PACK]),
+                op=ALU.mult,
+            )
+
+        def quantise_l(t):
+            nc.vector.quantize_mx(
+                out=l_codes[:, t, :].bitcast(FP8X4),
+                scales=l_scales[:, t, :],
+                in_=l_grouped[t][:].rearrange("p i u -> p (i u)"),
+            )
+
+        def turn_x(t):
+            x_words = x_sb[t][:].bitcast(F32)
+            turned[t] = ps_x.tile([P, PASSES * HALF, P], F32, name="turned")
+            for c in range(PASSES * HALF):
+                nc.tensor.transpose(turned[t][:, c, :], x_words[:, c * P : (c + 1) * P], ident[:])
+
+        def group_x(t):
+            nc.scalar.copy(out=x_grouped[t][:], in_=turned[t][:].rearrange("p (g u) n -> p g n u", u=HALF))
+
+        def quantise_x(t):
+            nc.vector.quantize_mx(
+                out=x_codes[:, t, :, :].rearrange("p g n -> p (g n)").bitcast(FP8X4),
+                scales=x_scales[:, t, :, :].rearrange("p g n -> p (g n)"),
+                in_=x_grouped[t][:].rearrange("p g n u -> p (g n u)").bitcast(BF16),
+            )
 
         adj_rows = adj.rearrange("(t p) j -> p t j", p=P)
-        adj_sb = keep.tile([P, TILES, NODES], BF16)
         for h in range(2):
             nc.sync.dma_start(out=adj_sb[:, 2 * h : 2 * h + 2, :], in_=adj_rows[:, 2 * h : 2 * h + 2, :])
-        w_sb = keep.tile([P, PASSES, PACK, F_OUT], BF16)
         nc.sync.dma_start(
             out=w_sb[:].rearrange("q g (u e) f -> q (g u) (e f)", e=2),
             in_=weight.rearrange("(c q e) f -> q c (e f)", q=P, e=2),
         )
         x_rows = x.rearrange("(t p) k -> p t k", p=P)
-        x_sb = []
         for t in range(TILES):
-            x_t = keep.tile([P, F_IN], BF16, name="x%d" % t)
-            nc.sync.dma_start(out=x_t[:], in_=x_rows[:, t, :])
-            x_sb.append(x_t)
+            nc.sync.dma_start(out=x_sb[t][:], in_=x_rows[:, t, :])
         bias_row = const.tile([P, F_OUT], BF16)
         nc.vector.memset(bias_row[:], 0.0)
         nc.scalar.dma_start(out=bias_row[0:1, :], in_=b.rearrange("(o f) -> o f", o=1))
@@ -59,82 +133,56 @@ def tile_graphconvolution_s_kernel(tc, x, adj, weight, b, out):
         warm = const.tile([P, 1], F32)
         nc.vector.memset(warm[:], 1.0)
         nc.scalar.activation(out=warm[:], in_=warm[:], func=ACT.Abs_reciprocal_sqrt)
-
-        bias_ps = ps_one.tile([P, F_OUT], F32)
+        bias_ps = ps_one.tile([P, F_OUT], F32, tag="late")
         nc.tensor.matmul(out=bias_ps[:], lhsT=ones[:], rhs=bias_row[:], start=True, stop=True)
         bias_sb = const.tile([P, F_OUT], F32)
         nc.scalar.copy(out=bias_sb[:], in_=bias_ps[:])
 
-        w_grouped = keep.tile([P, PASSES, F_OUT, PACK], BF16, align_bytes=64)
+        for t in range(TILES):
+            negate_and_sum(t)
+        diagonal = sharp[:].rearrange("p (t w) -> p t w", w=NODES + P)[:, :, 0:P]
+        nc.vector.scalar_tensor_tensor(
+            out=diagonal, in0=ident[:].unsqueeze(1).to_broadcast([P, TILES, P]), scalar=2.0, in1=diagonal,
+            op0=ALU.mult, op1=ALU.add,
+        )
+        nc.scalar.activation(
+            out=d[:].rearrange("p (h e) -> p e h", e=2), in_=neg_deg[:, :, 0:2],
+            func=ACT.Abs_reciprocal_sqrt, bias=2.0, scale=-1.0,
+        )
+
         nc.vector.tensor_copy(out=w_grouped[:], in_=w_sb[:].rearrange("q g t f -> q g f t"))
-        w_codes = keep.tile([P, PASSES, F_OUT], U32, align_bytes=64)
-        w_scales = keep.tile([P, PASSES, F_OUT], U8, align_bytes=64)
         nc.vector.quantize_mx(
             out=w_codes[:].rearrange("q g f -> q (g f)").bitcast(FP8X4),
             scales=w_scales[:].rearrange("q g f -> q (g f)"),
             in_=w_grouped[:].rearrange("q g f t -> q (g f t)"),
         )
 
-        sharp = []
+        turn_x(0)
+        turn_x(1)
         for t in range(TILES):
-            sharp.append(keep.tile([P, NODES], F32, name="sharp%d" % t))
-        neg_deg_v = keep.tile([P, 2], F32)
-        neg_deg_s = keep.tile([P, 2], F32)
-        for t in range(2):
-            nc.vector.tensor_scalar(
-                out=sharp[t][:], in0=adj_sb[:, t, :], scalar1=-1.0, scalar2=None,
-                op0=ALU.mult, op1=ALU.add, accum_out=neg_deg_v[:, t : t + 1],
-            )
-        for t in range(2, TILES):
-            nc.scalar.activation(
-                out=sharp[t][:], in_=adj_sb[:, t, :], func=ACT.Copy, scale=-1.0,
-                accum_out=neg_deg_s[:, t - 2 : t - 1],
-            )
-        for t in range(TILES):
-            diag = sharp[t][:, t * P : (t + 1) * P]
-            nc.vector.scalar_tensor_tensor(
-                out=diag, in0=ident[:], scalar=2.0, in1=diag, op0=ALU.mult, op1=ALU.add
-            )
-        d = keep.tile([P, TILES], F32)
-        nc.scalar.activation(out=d[:, 0:2], in_=neg_deg_v[:], func=ACT.Abs_reciprocal_sqrt, bias=2.0, scale=-1.0)
-        nc.scalar.activation(out=d[:, 2:4], in_=neg_deg_s[:], func=ACT.Abs_reciprocal_sqrt, bias=2.0, scale=-1.0)
-
-        l_codes = keep.tile([P, TILES, P], U32, align_bytes=64)
-        l_scales = keep.tile([P, TILES, P], U8, align_bytes=64)
-        for t in range(TILES):
-            nc.vector.tensor_scalar(
-                out=sharp[t][:], in0=sharp[t][:], scalar1=d[:, t : t + 1], scalar2=None, op0=ALU.mult
-            )
-            flipped = ps_l.tile([P, PACK, P], F32)
-            for u in range(PACK):
-                nc.tensor.transpose(flipped[:, u, :], sharp[t][:, u * P : (u + 1) * P], ident[:])
-            l_grouped = keep.tile([P, P, PACK], BF16, name="l_grouped%d" % t, align_bytes=64)
-            nc.vector.tensor_tensor(
-                out=l_grouped[:],
-                in0=flipped[:].rearrange("p u i -> p i u"),
-                in1=d[:].unsqueeze(1).to_broadcast([P, P, PACK]),
-                op=ALU.mult,
-            )
-            nc.vector.quantize_mx(
-                out=l_codes[:, t, :].bitcast(FP8X4),
-                scales=l_scales[:, t, :],
-                in_=l_grouped[:].rearrange("p i u -> p (i u)"),
-            )
-
-        x_codes = keep.tile([P, TILES, PASSES, P], U32, align_bytes=64)
-        x_scales = keep.tile([P, TILES, PASSES, P], U8, align_bytes=64)
-        for t in range(TILES):
-            x_words = x_sb[t][:].bitcast(F32)
-            turned = ps_x.tile([P, PASSES * HALF, P], F32)
-            for c in range(PASSES * HALF):
-                nc.tensor.transpose(turned[:, c, :], x_words[:, c * P : (c + 1) * P], ident[:])
-            x_grouped = keep.tile([P, PASSES, P, HALF], F32, name="x_grouped%d" % t, align_bytes=64)
-            nc.scalar.copy(out=x_grouped[:], in_=turned[:].rearrange("p (g u) n -> p g n u", u=HALF))
-            nc.vector.quantize_mx(
-                out=x_codes[:, t, :, :].rearrange("p g n -> p (g n)").bitcast(FP8X4),
-                scales=x_scales[:, t, :, :].rearrange("p g n -> p (g n)"),
-                in_=x_grouped[:].rearrange("p g n u -> p (g n u)").bitcast(BF16),
-            )
+            scale_rows(t)
+        flip_rows(0)
+        flip_rows(1)
+        group_x(0)
+        turn_x(2)
+        flip_rows(2)
+        scale_columns(0)
+        scale_columns(1)
+        group_x(1)
+        turn_x(3)
+        flip_rows(3)
+        group_x(2)
+        group_x(3)
+        quantise_l(0)
+        quantise_x(0)
+        quantise_l(1)
+        quantise_x(1)
+        quantise_x(2)
+        quantise_x(3)
+        scale_columns(2)
+        scale_columns(3)
+        quantise_l(2)
+        quantise_l(3)
 
         support = ps_one.tile([P, TILES, F_OUT], F32)
         for t in range(TILES):
@@ -158,7 +206,7 @@ def tile_graphconvolution_s_kernel(tc, x, adj, weight, b, out):
             in_=s_grouped[:].rearrange("p f t -> p (f t)"),
         )
 
-        product = ps_one.tile([P, TILES, F_OUT], F32)
+        product = ps_one.tile([P, TILES, F_OUT], F32, tag="late")
         for t in range(TILES):
             nc.tensor.matmul_mx(
                 out=product[:, t, :],

@@ -115,12 +115,14 @@ def tile_graphconvolution_s_kernel(tc, x, adj, weight, b, out):
         adj_rows = adj.rearrange("(t p) j -> p t j", p=P)
         for h in range(2):
             nc.sync.dma_start(out=adj_sb[:, 2 * h : 2 * h + 2, :], in_=adj_rows[:, 2 * h : 2 * h + 2, :])
+        x_rows = x.rearrange("(t p) k -> p t k", p=P)
+        for t in range(2):
+            nc.sync.dma_start(out=x_sb[t][:], in_=x_rows[:, t, :])
         nc.sync.dma_start(
             out=w_sb[:].rearrange("q g (u e) f -> q (g u) (e f)", e=2),
             in_=weight.rearrange("(c q e) f -> q c (e f)", q=P, e=2),
         )
-        x_rows = x.rearrange("(t p) k -> p t k", p=P)
-        for t in range(TILES):
+        for t in range(2, TILES):
             nc.sync.dma_start(out=x_sb[t][:], in_=x_rows[:, t, :])
         bias_row = const.tile([P, F_OUT], BF16)
         nc.vector.memset(bias_row[:], 0.0)
@@ -159,25 +161,27 @@ def tile_graphconvolution_s_kernel(tc, x, adj, weight, b, out):
 
         turn_x(0)
         turn_x(1)
-        for t in range(TILES):
-            scale_rows(t)
+        scale_rows(0)
+        scale_rows(1)
         flip_rows(0)
-        flip_rows(1)
         group_x(0)
+        scale_rows(2)
+        scale_rows(3)
         turn_x(2)
-        flip_rows(2)
-        scale_columns(0)
-        scale_columns(1)
+        flip_rows(1)
         group_x(1)
-        turn_x(3)
-        flip_rows(3)
-        group_x(2)
-        group_x(3)
-        quantise_l(0)
+        scale_columns(0)
         quantise_x(0)
-        quantise_l(1)
         quantise_x(1)
+        turn_x(3)
+        group_x(2)
+        flip_rows(2)
+        flip_rows(3)
+        group_x(3)
+        scale_columns(1)
+        quantise_l(0)
         quantise_x(2)
+        quantise_l(1)
         quantise_x(3)
         scale_columns(2)
         scale_columns(3)

from contextlib import ExitStack

import concourse.mybir as mybir
from concourse.masks import make_identity

F32 = mybir.dt.float32
BF16 = mybir.dt.bfloat16
U32 = mybir.dt.uint32
U8 = mybir.dt.uint8
FP8X4 = mybir.dt.float8_e4m3fn_x4
ACT = mybir.ActivationFunctionType
ALU = mybir.AluOpType

P = 128
PACK = 4
K_PASS = P * PACK
NODES = 512
F_IN = 1024
F_OUT = 128
TILES = NODES // P
PASSES = F_IN // K_PASS
HALF = 2

FLOPS = 2 * NODES * F_IN * F_OUT + 2 * NODES * NODES * F_OUT


def tile_graphconvolution_s_kernel(tc, x, adj, weight, b, out):
    nc = tc.nc
    with ExitStack() as stack:
        const = stack.enter_context(tc.tile_pool(name="const", bufs=1))
        keep = stack.enter_context(tc.tile_pool(name="keep", bufs=1))
        ps_x = stack.enter_context(tc.psum_pool(name="ps_x", bufs=3))
        ps_l = stack.enter_context(tc.psum_pool(name="ps_l", bufs=3))
        ps_one = stack.enter_context(tc.psum_pool(name="ps_one", bufs=1))
        stack.enter_context(tc.manual_schedule())

        adj_sb = keep.tile([P, TILES, NODES], BF16)
        w_sb = keep.tile([P, PASSES, PACK, F_OUT], BF16)
        x_sb = [keep.tile([P, F_IN], BF16, name="x%d" % t) for t in range(TILES)]
        sharp = keep.tile([P, TILES * (NODES + P)], F32)
        neg_deg = keep.tile([P, 2, 8], F32)
        d = keep.tile([P, TILES], F32)
        w_grouped = keep.tile([P, PASSES, F_OUT, PACK], BF16, align_bytes=64)
        w_codes = keep.tile([P, PASSES, F_OUT], U32, align_bytes=64)
        w_scales = keep.tile([P, PASSES, F_OUT], U8, align_bytes=64)
        x_grouped = [keep.tile([P, PASSES, P, HALF], F32, name="x_grouped%d" % t, align_bytes=64) for t in range(TILES)]
        x_codes = keep.tile([P, TILES, PASSES, P], U32, align_bytes=64)
        x_scales = keep.tile([P, TILES, PASSES, P], U8, align_bytes=64)
        l_grouped = [keep.tile([P, P, PACK], BF16, name="l_grouped%d" % t, align_bytes=64) for t in range(TILES)]
        l_codes = keep.tile([P, TILES, P], U32, align_bytes=64)
        l_scales = keep.tile([P, TILES, P], U8, align_bytes=64)
        turned = {}
        flipped = {}

        def row_tile(t):
            return sharp[:, t * NODES : (t + 1) * NODES]

        def negate_and_sum(t):
            if t % 2 == 0:
                nc.vector.tensor_scalar(
                    out=row_tile(t), in0=adj_sb[:, t, :], scalar1=-1.0, scalar2=None,
                    op0=ALU.mult, op1=ALU.add, accum_out=neg_deg[:, 0, t // 2 : t // 2 + 1],
                )
            else:
                nc.scalar.activation(
                    out=row_tile(t), in_=adj_sb[:, t, :], func=ACT.Copy, scale=-1.0,
                    accum_out=neg_deg[:, 1, t // 2 : t // 2 + 1],
                )

        def scale_rows(t):
            if t % 2 == 0:
                nc.scalar.activation(out=row_tile(t), in_=row_tile(t), func=ACT.Copy, scale=d[:, t : t + 1])
            else:
                nc.gpsimd.tensor_scalar(
                    out=row_tile(t), in0=row_tile(t), scalar1=d[:, t : t + 1], scalar2=1.0,
                    op0=ALU.mult, op1=ALU.mult,
                )

        def flip_rows(t):
            flipped[t] = ps_l.tile([P, PACK, P], F32, name="flipped")
            for u in range(PACK):
                nc.tensor.transpose(flipped[t][:, u, :], row_tile(t)[:, u * P : (u + 1) * P], ident[:])

        def scale_columns(t):
            nc.vector.tensor_tensor(
                out=l_grouped[t][:],
                in0=flipped[t][:].rearrange("p u i -> p i u"),
                in1=d[:].unsqueeze(1).to_broadcast([P, P, PACK]),
                op=ALU.mult,
            )

        def quantise_l(t):
            nc.vector.quantize_mx(
                out=l_codes[:, t, :].bitcast(FP8X4),
                scales=l_scales[:, t, :],
                in_=l_grouped[t][:].rearrange("p i u -> p (i u)"),
            )

        def turn_x(t):
            x_words = x_sb[t][:].bitcast(F32)
            turned[t] = ps_x.tile([P, PASSES * HALF, P], F32, name="turned")
            for c in range(PASSES * HALF):
                nc.tensor.transpose(turned[t][:, c, :], x_words[:, c * P : (c + 1) * P], ident[:])

        def group_x(t):
            nc.scalar.copy(out=x_grouped[t][:], in_=turned[t][:].rearrange("p (g u) n -> p g n u", u=HALF))

        def quantise_x(t):
            nc.vector.quantize_mx(
                out=x_codes[:, t, :, :].rearrange("p g n -> p (g n)").bitcast(FP8X4),
                scales=x_scales[:, t, :, :].rearrange("p g n -> p (g n)"),
                in_=x_grouped[t][:].rearrange("p g n u -> p (g n u)").bitcast(BF16),
            )

        adj_rows = adj.rearrange("(t p) j -> p t j", p=P)
        for h in range(2):
            nc.sync.dma_start(out=adj_sb[:, 2 * h : 2 * h + 2, :], in_=adj_rows[:, 2 * h : 2 * h + 2, :])
        x_rows = x.rearrange("(t p) k -> p t k", p=P)
        for t in range(2):
            nc.sync.dma_start(out=x_sb[t][:], in_=x_rows[:, t, :])
        nc.sync.dma_start(
            out=w_sb[:].rearrange("q g (u e) f -> q (g u) (e f)", e=2),
            in_=weight.rearrange("(c q e) f -> q c (e f)", q=P, e=2),
        )
        for t in range(2, TILES):
            nc.sync.dma_start(out=x_sb[t][:], in_=x_rows[:, t, :])
        bias_row = const.tile([P, F_OUT], BF16)
        nc.vector.memset(bias_row[:], 0.0)
        nc.scalar.dma_start(out=bias_row[0:1, :], in_=b.rearrange("(o f) -> o f", o=1))

        ident = const.tile([P, P], F32)
        make_identity(nc, ident[:])
        ones = const.tile([P, P], BF16)
        nc.vector.memset(ones[:], 1.0)
        warm = const.tile([P, 1], F32)
        nc.vector.memset(warm[:], 1.0)
        nc.scalar.activation(out=warm[:], in_=warm[:], func=ACT.Abs_reciprocal_sqrt)
        bias_ps = ps_one.tile([P, F_OUT], F32, tag="late")
        nc.tensor.matmul(out=bias_ps[:], lhsT=ones[:], rhs=bias_row[:], start=True, stop=True)
        bias_sb = const.tile([P, F_OUT], F32)
        nc.scalar.copy(out=bias_sb[:], in_=bias_ps[:])

        for t in range(TILES):
            negate_and_sum(t)
        diagonal = sharp[:].rearrange("p (t w) -> p t w", w=NODES + P)[:, :, 0:P]
        nc.vector.scalar_tensor_tensor(
            out=diagonal, in0=ident[:].unsqueeze(1).to_broadcast([P, TILES, P]), scalar=2.0, in1=diagonal,
            op0=ALU.mult, op1=ALU.add,
        )
        nc.scalar.activation(
            out=d[:].rearrange("p (h e) -> p e h", e=2), in_=neg_deg[:, :, 0:2],
            func=ACT.Abs_reciprocal_sqrt, bias=2.0, scale=-1.0,
        )

        nc.vector.tensor_copy(out=w_grouped[:], in_=w_sb[:].rearrange("q g t f -> q g f t"))
        nc.vector.quantize_mx(
            out=w_codes[:].rearrange("q g f -> q (g f)").bitcast(FP8X4),
            scales=w_scales[:].rearrange("q g f -> q (g f)"),
            in_=w_grouped[:].rearrange("q g f t -> q (g f t)"),
        )

        turn_x(0)
        turn_x(1)
        scale_rows(0)
        scale_rows(1)
        flip_rows(0)
        group_x(0)
        scale_rows(2)
        scale_rows(3)
        turn_x(2)
        flip_rows(1)
        group_x(1)
        scale_columns(0)
        quantise_x(0)
        quantise_x(1)
        turn_x(3)
        group_x(2)
        flip_rows(2)
        flip_rows(3)
        group_x(3)
        scale_columns(1)
        quantise_l(0)
        quantise_x(2)
        quantise_l(1)
        quantise_x(3)
        scale_columns(2)
        scale_columns(3)
        quantise_l(2)
        quantise_l(3)

        support = ps_one.tile([P, TILES, F_OUT], F32)
        for t in range(TILES):
            for g in range(PASSES):
                nc.tensor.matmul_mx(
                    out=support[:, t, :],
                    lhsT=x_codes[:, t, g, :].bitcast(FP8X4),
                    lhsT_scale=x_scales[:, t, g, :],
                    rhs=w_codes[:, g, :].bitcast(FP8X4),
                    rhs_scale=w_scales[:, g, :],
                    start=(g == 0),
                    stop=(g == PASSES - 1),
                )
        s_grouped = keep.tile([P, F_OUT, PACK], BF16, align_bytes=64)
        nc.scalar.copy(out=s_grouped[:], in_=support[:].rearrange("p t f -> p f t"))
        s_codes = keep.tile([P, F_OUT], U32, align_bytes=64)
        s_scales = keep.tile([P, F_OUT], U8, align_bytes=64)
        nc.vector.quantize_mx(
            out=s_codes[:].bitcast(FP8X4),
            scales=s_scales[:],
            in_=s_grouped[:].rearrange("p f t -> p (f t)"),
        )

        product = ps_one.tile([P, TILES, F_OUT], F32, tag="late")
        for t in range(TILES):
            nc.tensor.matmul_mx(
                out=product[:, t, :],
                lhsT=l_codes[:, t, :].bitcast(FP8X4),
                lhsT_scale=l_scales[:, t, :],
                rhs=s_codes[:].bitcast(FP8X4),
                rhs_scale=s_scales[:],
                start=True,
                stop=True,
            )
        result = keep.tile([P, TILES, F_OUT], F32)
        nc.vector.tensor_tensor(
            out=result[:], in0=product[:], in1=bias_sb[:].unsqueeze(1).to_broadcast([P, TILES, F_OUT]), op=ALU.add
        )
        nc.vector.tensor_scalar_max(out=result[:], in0=result[:], scalar1=0.0)
        nc.sync.dma_start(out=out.rearrange("(t p) f -> p t f", p=P), in_=result[:])
